import numpy as np
import ml_dtypes


def mxq(x, axis, fmt="e4m3"):
    dtype, down = {"e4m3": (ml_dtypes.float8_e4m3fn, 7), "e5m2": (ml_dtypes.float8_e5m2, 14)}[fmt]
    v = np.moveaxis(np.asarray(x, np.float32).astype(ml_dtypes.bfloat16).astype(np.float64), axis, -1)
    blocks = v.reshape(v.shape[:-1] + (-1, 32))
    amax = np.abs(blocks).max(-1, keepdims=True)
    byte = np.maximum(np.where(amax > 0, np.frexp(amax)[1] - 1 + 127, 0) - down, 1)
    scale = np.exp2(byte - 127.0)
    codes = (blocks / scale).astype(np.float32).astype(dtype).astype(np.float64)
    return np.moveaxis((codes * scale).reshape(v.shape), -1, axis)


WIDE = False


def mx_kscale(k):
    if not WIDE:
        return np.ones(k)
    levels = np.array([10, -10, 5, -5, 0])
    a = np.random.permutation(np.resize(levels, k // 512 * 4)).reshape(k // 512, 4)
    idx = np.arange(k)
    return np.exp2(a[idx // 512, idx % 128 // 32])


BF16 = ml_dtypes.bfloat16


def bf(x):
    return np.asarray(x, np.float32).astype(BF16)


def f64(x):
    return np.asarray(x).astype(np.float64)


M, K, N = 8192, 512, 512
BITS = 8


def setup_inputs():
    s = mx_kscale(K)
    return {"x": bf(np.random.standard_normal((M, K)) * s),
            "qw": bf(np.random.randint(0, 2 ** BITS, (N, K)) / s),
            "scale": bf(np.random.uniform(0.01, 0.02, 1) / np.sqrt(K)),
            "zero_point": bf(np.random.uniform(0.375, 0.625, 1) * 2 ** BITS / s.max()),
            "bias": bf(np.random.standard_normal(N))}


def reference(x, qw, scale, zero_point, bias):
    w = (f64(qw) - f64(zero_point)) * f64(scale)
    return (mxq(f64(x), 1, "e4m3") @ mxq(w, 1, "e4m3").T) + f64(bias)

@@ -1,0 +1,167 @@
+from contextlib import ExitStack
+
+import concourse.mybir as mybir
+from concourse.masks import make_identity
+
+F32 = mybir.dt.float32
+BF16 = mybir.dt.bfloat16
+U32 = mybir.dt.uint32
+U8 = mybir.dt.uint8
+FP8X4 = mybir.dt.float8_e4m3fn_x4
+ALU = mybir.AluOpType
+
+P = 128
+M, K, N = 8192, 512, 512
+FLOPS = 2 * M * K * N
+TILES = M // P
+GROUP = 4
+ROUNDS = TILES // GROUP
+AHEAD = 2
+X_CHUNKS = [4, 4, 8, 16, 16, 16]
+KW = K // 2
+
+
+def tile_quantizedlinear_t_kernel(tc, x, qw, scale, zero_point, bias, out):
+    nc = tc.nc
+    x2 = x.rearrange("(p t) k -> p (t k)", t=TILES)
+    out2 = out.rearrange("(p t) n -> p (t n)", t=TILES)
+    with ExitStack() as ctx:
+        ctx.enter_context(tc.manual_schedule())
+        keep = ctx.enter_context(tc.tile_pool(name="keep", bufs=1))
+        gpool = ctx.enter_context(tc.tile_pool(name="gpool", bufs=3))
+        cpool = ctx.enter_context(tc.tile_pool(name="cpool", bufs=3))
+        opool = ctx.enter_context(tc.tile_pool(name="opool", bufs=10))
+        ps_t = ctx.enter_context(tc.psum_pool(name="ps_t", bufs=4))
+        ps_o = ctx.enter_context(tc.psum_pool(name="ps_o", bufs=4))
+
+        ident = keep.tile([P, P], F32, name="ident")
+        make_identity(nc, ident[:])
+        ones = keep.tile([P, P], BF16, name="ones")
+        nc.vector.memset(ones[:], 1.0)
+        srow = keep.tile([P, 32], BF16, name="srow")
+        nc.vector.memset(srow[:], 0.0)
+        brow = keep.tile([P, N], BF16, name="brow")
+        nc.vector.memset(brow[:], 0.0)
+        nc.scalar.dma_start(out=srow[0:1, 0:1], in_=scale.unsqueeze(0))
+        nc.scalar.dma_start(out=srow[0:1, 16:17], in_=zero_point.unsqueeze(0))
+        nc.scalar.dma_start(out=brow[0:1, :], in_=bias.unsqueeze(0))
+
+        q_sb = keep.tile([P, 4 * K], BF16, name="q_sb")
+        nc.sync.dma_start(
+            out=q_sb[:].rearrange("p (j k) -> p j k", j=4),
+            in_=qw.rearrange("(j p) k -> p j k", p=P),
+        )
+        x_words = []
+        t0 = 0
+        for ci, cnt in enumerate(X_CHUNKS):
+            x_sb = keep.tile([P, cnt * K], BF16, name="x_sb%d" % ci)
+            nc.sync.dma_start(out=x_sb[:], in_=x2[:, t0 * K : (t0 + cnt) * K])
+            xw = x_sb[:].bitcast(F32)
+            for i in range(cnt):
+                x_words.append(xw[:, i * KW : (i + 1) * KW])
+            t0 += cnt
+
+        sz_ps = ps_o.tile([P, 32], F32, name="sz_ps", tag="acc")
+        nc.tensor.matmul(sz_ps[:], lhsT=ones[:], rhs=srow[:], start=True, stop=True)
+        sz = keep.tile([P, 32], F32, name="sz")
+        nc.vector.tensor_copy(out=sz[:], in_=sz_ps[:])
+
+        q_words = q_sb[:].bitcast(F32)
+        w_grp = keep.tile([P, 4 * N], BF16, name="w_grp", align_bytes=64)
+        for h in range(2):
+            wt = ps_t.tile([P, 512], F32, name="wt", tag="tp")
+            for j in range(2):
+                for u in range(2):
+                    c0 = (2 * h + j) * KW + u * P
+                    nc.tensor.transpose(
+                        wt[:, u * 256 + j * P : u * 256 + (j + 1) * P],
+                        q_words[:, c0 : c0 + P],
+                        ident[:],
+                    )
+            nc.vector.tensor_scalar(
+                out=w_grp[:, h * 1024 : (h + 1) * 1024].rearrange(
+                    "p (n u e) -> p n u e", u=2, e=2
+                ),
+                in0=wt[:].bitcast(BF16).rearrange("p (u n e) -> p n u e", u=2, e=2),
+                scalar1=sz[:, 16:17],
+                scalar2=sz[:, 0:1],
+                op0=ALU.subtract,
+                op1=ALU.mult,
+            )
+        w_codes = keep.tile([P, N], U32, name="w_codes", align_bytes=64)
+        w_scales = keep.tile([P, N], U8, name="w_scales", align_bytes=64)
+        nc.vector.quantize_mx(
+            out=w_codes[:].bitcast(FP8X4), scales=w_scales[:], in_=w_grp[:]
+        )
+
+        b_ps = ps_o.tile([P, N], F32, name="b_ps", tag="acc")
+        nc.tensor.matmul(b_ps[:], lhsT=ones[:], rhs=brow[:], start=True, stop=True)
+        bias_sb = keep.tile([P, N], F32, name="bias_sb")
+        nc.scalar.copy(out=bias_sb[:], in_=b_ps[:])
+
+        grouped = {}
+        codes = {}
+
+        def transposes(g):
+            grp = gpool.tile([P, GROUP * K], BF16, name="grp", align_bytes=64)
+            grouped[g] = grp
+            grp_w = grp[:].bitcast(F32)
+            for h in range(GROUP // 2):
+                xt = ps_t.tile([P, 512], F32, name="xt", tag="tp")
+                for j in range(2):
+                    xw = x_words[g * GROUP + 2 * h + j]
+                    for u in range(2):
+                        nc.tensor.transpose(
+                            xt[:, u * 256 + j * P : u * 256 + (j + 1) * P],
+                            xw[:, u * P : (u + 1) * P],
+                            ident[:],
+                        )
+                nc.scalar.copy(
+                    out=grp_w[:, h * 512 : (h + 1) * 512].rearrange(
+                        "p (r u) -> p r u", u=2
+                    ),
+                    in_=xt[:].rearrange("p (u r) -> p r u", u=2),
+                )
+
+        def quantise(g):
+            cw = cpool.tile([P, GROUP * P], U32, name="cw", align_bytes=64)
+            cs = cpool.tile([P, GROUP * P], U8, name="cs", align_bytes=64)
+            codes[g] = (cw, cs)
+            nc.vector.quantize_mx(
+                out=cw[:].bitcast(FP8X4), scales=cs[:], in_=grouped[g][:]
+            )
+
+        for g in range(AHEAD):
+            transposes(g)
+        quantise(0)
+
+        for g in range(ROUNDS):
+            if g + AHEAD < ROUNDS:
+                transposes(g + AHEAD)
+            cw, cs = codes[g]
+            accs = []
+            for j in range(GROUP):
+                acc = ps_o.tile([P, N], F32, name="acc", tag="acc")
+                accs.append(acc)
+                nc.tensor.matmul_mx(
+                    out=acc[:],
+                    lhsT=cw[:, j * P : (j + 1) * P].bitcast(FP8X4),
+                    lhsT_scale=cs[:, j * P : (j + 1) * P],
+                    rhs=w_codes[:].bitcast(FP8X4),
+                    rhs_scale=w_scales[:],
+                    start=True,
+                    stop=True,
+                )
+            if g + 1 < ROUNDS:
+                quantise(g + 1)
+            o_sb = opool.tile([P, GROUP * N], F32, name="o_sb")
+            for j in range(GROUP):
+                nc.vector.tensor_tensor(
+                    out=o_sb[:, j * N : (j + 1) * N],
+                    in0=accs[j][:],
+                    in1=bias_sb[:],
+                    op=ALU.add,
+                )
+            nc.sync.dma_start(
+                out=out2[:, g * GROUP * N : (g + 1) * GROUP * N], in_=o_sb[:]
+            )

@@ -17,7 +17,9 @@ TILES = M // P
 GROUP = 4
 ROUNDS = TILES // GROUP
 AHEAD = 2
-X_CHUNKS = [4, 4, 8, 16, 16, 16]
+X_CHUNKS = [4, 4, 8, 16, 32]
+STORE_ROUNDS = [2, 2, 2, 2, 2, 2, 2, 1, 1]
+SCALAR_BANKS = (3,)
 KW = K // 2
 
 
@@ -30,21 +32,22 @@ def tile_quantizedlinear_t_kernel(tc, x, qw, scale, zero_point, bias, out):
         keep = ctx.enter_context(tc.tile_pool(name="keep", bufs=1))
         gpool = ctx.enter_context(tc.tile_pool(name="gpool", bufs=3))
         cpool = ctx.enter_context(tc.tile_pool(name="cpool", bufs=3))
-        opool = ctx.enter_context(tc.tile_pool(name="opool", bufs=10))
+        opool = ctx.enter_context(tc.tile_pool(name="opool", bufs=5))
         ps_t = ctx.enter_context(tc.psum_pool(name="ps_t", bufs=4))
         ps_o = ctx.enter_context(tc.psum_pool(name="ps_o", bufs=4))
 
+        sz_bf = keep.tile([P, 2, 16], BF16, name="sz_bf")
+        with nc.allow_non_contiguous_dma(reason="one bfloat16 number for each partition"):
+            nc.scalar.dma_start(out=sz_bf[:, 0, 0:1], in_=scale.partition_broadcast(P))
+            nc.scalar.dma_start(
+                out=sz_bf[:, 1, 0:1], in_=zero_point.partition_broadcast(P)
+            )
         ident = keep.tile([P, P], F32, name="ident")
         make_identity(nc, ident[:])
-        ones = keep.tile([P, P], BF16, name="ones")
-        nc.vector.memset(ones[:], 1.0)
-        srow = keep.tile([P, 32], BF16, name="srow")
-        nc.vector.memset(srow[:], 0.0)
         brow = keep.tile([P, N], BF16, name="brow")
         nc.vector.memset(brow[:], 0.0)
-        nc.scalar.dma_start(out=srow[0:1, 0:1], in_=scale.unsqueeze(0))
-        nc.scalar.dma_start(out=srow[0:1, 16:17], in_=zero_point.unsqueeze(0))
-        nc.scalar.dma_start(out=brow[0:1, :], in_=bias.unsqueeze(0))
+        ones = keep.tile([P, P], BF16, name="ones")
+        nc.vector.memset(ones[:], 1.0)
 
         q_sb = keep.tile([P, 4 * K], BF16, name="q_sb")
         nc.sync.dma_start(
@@ -56,15 +59,15 @@ def tile_quantizedlinear_t_kernel(tc, x, qw, scale, zero_point, bias, out):
         for ci, cnt in enumerate(X_CHUNKS):
             x_sb = keep.tile([P, cnt * K], BF16, name="x_sb%d" % ci)
             nc.sync.dma_start(out=x_sb[:], in_=x2[:, t0 * K : (t0 + cnt) * K])
+            if ci == 0:
+                nc.sync.dma_start(out=brow[0:1, :], in_=bias.unsqueeze(0))
             xw = x_sb[:].bitcast(F32)
             for i in range(cnt):
                 x_words.append(xw[:, i * KW : (i + 1) * KW])
             t0 += cnt
 
-        sz_ps = ps_o.tile([P, 32], F32, name="sz_ps", tag="acc")
-        nc.tensor.matmul(sz_ps[:], lhsT=ones[:], rhs=srow[:], start=True, stop=True)
-        sz = keep.tile([P, 32], F32, name="sz")
-        nc.vector.tensor_copy(out=sz[:], in_=sz_ps[:])
+        sz = keep.tile([P, 2, 1], F32, name="sz")
+        nc.vector.tensor_copy(out=sz[:], in_=sz_bf[:, :, 0:1])
 
         q_words = q_sb[:].bitcast(F32)
         w_grp = keep.tile([P, 4 * N], BF16, name="w_grp", align_bytes=64)
@@ -83,8 +86,8 @@ def tile_quantizedlinear_t_kernel(tc, x, qw, scale, zero_point, bias, out):
                     "p (n u e) -> p n u e", u=2, e=2
                 ),
                 in0=wt[:].bitcast(BF16).rearrange("p (u n e) -> p n u e", u=2, e=2),
-                scalar1=sz[:, 16:17],
-                scalar2=sz[:, 0:1],
+                scalar1=sz[:, 1, :],
+                scalar2=sz[:, 0, :],
                 op0=ALU.subtract,
                 op1=ALU.mult,
             )
@@ -135,6 +138,10 @@ def tile_quantizedlinear_t_kernel(tc, x, qw, scale, zero_point, bias, out):
             transposes(g)
         quantise(0)
 
+        store_i = 0
+        store_first = 0
+        store_cnt = 0
+        o_sb = None
         for g in range(ROUNDS):
             if g + AHEAD < ROUNDS:
                 transposes(g + AHEAD)
@@ -154,14 +161,30 @@ def tile_quantizedlinear_t_kernel(tc, x, qw, scale, zero_point, bias, out):
                 )
             if g + 1 < ROUNDS:
                 quantise(g + 1)
-            o_sb = opool.tile([P, GROUP * N], F32, name="o_sb")
+            if g == store_first:
+                store_cnt = STORE_ROUNDS[store_i]
+                o_sb = opool.tile([P, store_cnt * GROUP * N], F32, name="o_sb")
             for j in range(GROUP):
-                nc.vector.tensor_tensor(
-                    out=o_sb[:, j * N : (j + 1) * N],
-                    in0=accs[j][:],
-                    in1=bias_sb[:],
-                    op=ALU.add,
+                c0 = ((g - store_first) * GROUP + j) * N
+                if j in SCALAR_BANKS:
+                    nc.scalar.copy(out=o_sb[:, c0 : c0 + N], in_=accs[j][:])
+                    nc.gpsimd.tensor_tensor(
+                        out=o_sb[:, c0 : c0 + N],
+                        in0=o_sb[:, c0 : c0 + N],
+                        in1=bias_sb[:],
+                        op=ALU.add,
+                    )
+                else:
+                    nc.vector.tensor_tensor(
+                        out=o_sb[:, c0 : c0 + N],
+                        in0=accs[j][:],
+                        in1=bias_sb[:],
+                        op=ALU.add,
+                    )
+            if g == store_first + store_cnt - 1:
+                nc.sync.dma_start(
+                    out=out2[:, store_first * GROUP * N : (g + 1) * GROUP * N],
+                    in_=o_sb[:],
                 )
-            nc.sync.dma_start(
-                out=out2[:, g * GROUP * N : (g + 1) * GROUP * N], in_=o_sb[:]
-            )
+                store_first = g + 1
+                store_i += 1

@@ -36,38 +36,37 @@ def tile_quantizedlinear_t_kernel(tc, x, qw, scale, zero_point, bias, out):
         ps_t = ctx.enter_context(tc.psum_pool(name="ps_t", bufs=4))
         ps_o = ctx.enter_context(tc.psum_pool(name="ps_o", bufs=4))
 
-        sz_bf = keep.tile([P, 2, 16], BF16, name="sz_bf")
-        with nc.allow_non_contiguous_dma(reason="one bfloat16 number for each partition"):
-            nc.scalar.dma_start(out=sz_bf[:, 0, 0:1], in_=scale.partition_broadcast(P))
-            nc.scalar.dma_start(
-                out=sz_bf[:, 1, 0:1], in_=zero_point.partition_broadcast(P)
-            )
-        ident = keep.tile([P, P], F32, name="ident")
-        make_identity(nc, ident[:])
+        srow = keep.tile([P, 64], BF16, name="srow")
+        nc.vector.memset(srow[:], 0.0)
         brow = keep.tile([P, N], BF16, name="brow")
         nc.vector.memset(brow[:], 0.0)
         ones = keep.tile([P, P], BF16, name="ones")
         nc.vector.memset(ones[:], 1.0)
+        ident = keep.tile([P, P], F32, name="ident")
+        make_identity(nc, ident[:])
 
         q_sb = keep.tile([P, 4 * K], BF16, name="q_sb")
         nc.sync.dma_start(
             out=q_sb[:].rearrange("p (j k) -> p j k", j=4),
             in_=qw.rearrange("(j p) k -> p j k", p=P),
         )
+        nc.sync.dma_start(out=srow[0:1, 0:1], in_=scale.unsqueeze(0))
+        nc.sync.dma_start(out=srow[0:1, 32:33], in_=zero_point.unsqueeze(0))
+        nc.sync.dma_start(out=brow[0:1, :], in_=bias.unsqueeze(0))
         x_words = []
         t0 = 0
         for ci, cnt in enumerate(X_CHUNKS):
             x_sb = keep.tile([P, cnt * K], BF16, name="x_sb%d" % ci)
             nc.sync.dma_start(out=x_sb[:], in_=x2[:, t0 * K : (t0 + cnt) * K])
-            if ci == 0:
-                nc.sync.dma_start(out=brow[0:1, :], in_=bias.unsqueeze(0))
             xw = x_sb[:].bitcast(F32)
             for i in range(cnt):
                 x_words.append(xw[:, i * KW : (i + 1) * KW])
             t0 += cnt
 
-        sz = keep.tile([P, 2, 1], F32, name="sz")
-        nc.vector.tensor_copy(out=sz[:], in_=sz_bf[:, :, 0:1])
+        sz_ps = ps_o.tile([P, 64], F32, name="sz_ps", tag="acc")
+        nc.tensor.matmul(sz_ps[:], lhsT=ones[:], rhs=srow[:], start=True, stop=True)
+        sz = keep.tile([P, 64], F32, name="sz")
+        nc.vector.tensor_copy(out=sz[:], in_=sz_ps[:])
 
         q_words = q_sb[:].bitcast(F32)
         w_grp = keep.tile([P, 4 * N], BF16, name="w_grp", align_bytes=64)
@@ -86,8 +85,8 @@ def tile_quantizedlinear_t_kernel(tc, x, qw, scale, zero_point, bias, out):
                     "p (n u e) -> p n u e", u=2, e=2
                 ),
                 in0=wt[:].bitcast(BF16).rearrange("p (u n e) -> p n u e", u=2, e=2),
-                scalar1=sz[:, 1, :],
-                scalar2=sz[:, 0, :],
+                scalar1=sz[:, 32:33],
+                scalar2=sz[:, 0:1],
                 op0=ALU.subtract,
                 op1=ALU.mult,
             )

@@ -18,7 +18,7 @@ GROUP = 4
 ROUNDS = TILES // GROUP
 AHEAD = 2
 X_CHUNKS = [4, 4, 8, 16, 32]
-STORE_ROUNDS = [2, 2, 2, 2, 2, 2, 2, 1, 1]
+STORE_TILES = [8, 8, 8, 8, 8, 8, 8, 4, 2, 1, 1]
 SCALAR_BANKS = (3,)
 KW = K // 2
 
@@ -32,12 +32,12 @@ def tile_quantizedlinear_t_kernel(tc, x, qw, scale, zero_point, bias, out):
         keep = ctx.enter_context(tc.tile_pool(name="keep", bufs=1))
         gpool = ctx.enter_context(tc.tile_pool(name="gpool", bufs=3))
         cpool = ctx.enter_context(tc.tile_pool(name="cpool", bufs=3))
-        opool = ctx.enter_context(tc.tile_pool(name="opool", bufs=5))
+        opool = ctx.enter_context(tc.tile_pool(name="opool", bufs=7))
         ps_t = ctx.enter_context(tc.psum_pool(name="ps_t", bufs=4))
         ps_o = ctx.enter_context(tc.psum_pool(name="ps_o", bufs=4))
 
         srow = keep.tile([P, 64], BF16, name="srow")
-        nc.vector.memset(srow[:], 0.0)
+        nc.gpsimd.memset(srow[:], 0.0)
         brow = keep.tile([P, N], BF16, name="brow")
         nc.vector.memset(brow[:], 0.0)
         ones = keep.tile([P, P], BF16, name="ones")
@@ -52,12 +52,13 @@ def tile_quantizedlinear_t_kernel(tc, x, qw, scale, zero_point, bias, out):
         )
         nc.sync.dma_start(out=srow[0:1, 0:1], in_=scale.unsqueeze(0))
         nc.sync.dma_start(out=srow[0:1, 32:33], in_=zero_point.unsqueeze(0))
-        nc.sync.dma_start(out=brow[0:1, :], in_=bias.unsqueeze(0))
         x_words = []
         t0 = 0
         for ci, cnt in enumerate(X_CHUNKS):
             x_sb = keep.tile([P, cnt * K], BF16, name="x_sb%d" % ci)
             nc.sync.dma_start(out=x_sb[:], in_=x2[:, t0 * K : (t0 + cnt) * K])
+            if ci == 0:
+                nc.sync.dma_start(out=brow[0:1, :], in_=bias.unsqueeze(0))
             xw = x_sb[:].bitcast(F32)
             for i in range(cnt):
                 x_words.append(xw[:, i * KW : (i + 1) * KW])
@@ -160,12 +161,13 @@ def tile_quantizedlinear_t_kernel(tc, x, qw, scale, zero_point, bias, out):
                 )
             if g + 1 < ROUNDS:
                 quantise(g + 1)
-            if g == store_first:
-                store_cnt = STORE_ROUNDS[store_i]
-                o_sb = opool.tile([P, store_cnt * GROUP * N], F32, name="o_sb")
             for j in range(GROUP):
-                c0 = ((g - store_first) * GROUP + j) * N
-                if j in SCALAR_BANKS:
+                t = g * GROUP + j
+                if t == store_first:
+                    store_cnt = STORE_TILES[store_i]
+                    o_sb = opool.tile([P, store_cnt * N], F32, name="o_sb")
+                c0 = (t - store_first) * N
+                if j in SCALAR_BANKS and g < ROUNDS - 1:
                     nc.scalar.copy(out=o_sb[:, c0 : c0 + N], in_=accs[j][:])
                     nc.gpsimd.tensor_tensor(
                         out=o_sb[:, c0 : c0 + N],
@@ -180,10 +182,9 @@ def tile_quantizedlinear_t_kernel(tc, x, qw, scale, zero_point, bias, out):
                         in1=bias_sb[:],
                         op=ALU.add,
                     )
-            if g == store_first + store_cnt - 1:
-                nc.sync.dma_start(
-                    out=out2[:, store_first * GROUP * N : (g + 1) * GROUP * N],
-                    in_=o_sb[:],
-                )
-                store_first = g + 1
-                store_i += 1
+                if t == store_first + store_cnt - 1:
+                    nc.sync.dma_start(
+                        out=out2[:, store_first * N : (t + 1) * N], in_=o_sb[:]
+                    )
+                    store_first = t + 1
+                    store_i += 1

@@ -13,178 +13,184 @@ ALU = mybir.AluOpType
 P = 128
 M, K, N = 8192, 512, 512
 FLOPS = 2 * M * K * N
-TILES = M // P
-GROUP = 4
-ROUNDS = TILES // GROUP
+PACK = 4
+WORDS = K // 2
+HALF = 2 * P
+ROW_TILES = M // P
+ROUND = 4
+ROUNDS = ROW_TILES // ROUND
 AHEAD = 2
-X_CHUNKS = [4, 4, 8, 16, 32]
-STORE_TILES = [8, 8, 8, 8, 8, 8, 8, 4, 2, 1, 1]
-SCALAR_BANKS = (3,)
-KW = K // 2
+SCALAR_BANK = ROUND - 1
+X_LOADS = (4, 4, 8, 16, 32)
+STORE_ROUNDS = 2
+SCALE_COL, ZERO_POINT_COL, DEQUANT_COLS = 0, 32, 64
 
 
 def tile_quantizedlinear_t_kernel(tc, x, qw, scale, zero_point, bias, out):
     nc = tc.nc
-    x2 = x.rearrange("(p t) k -> p (t k)", t=TILES)
-    out2 = out.rearrange("(p t) n -> p (t n)", t=TILES)
+    x_runs = x.rearrange("(p t) k -> p (t k)", t=ROW_TILES)
+    out_runs = out.rearrange("(p t) n -> p (t n)", t=ROW_TILES)
+
     with ExitStack() as ctx:
         ctx.enter_context(tc.manual_schedule())
         keep = ctx.enter_context(tc.tile_pool(name="keep", bufs=1))
-        gpool = ctx.enter_context(tc.tile_pool(name="gpool", bufs=3))
-        cpool = ctx.enter_context(tc.tile_pool(name="cpool", bufs=3))
-        opool = ctx.enter_context(tc.tile_pool(name="opool", bufs=7))
-        ps_t = ctx.enter_context(tc.psum_pool(name="ps_t", bufs=4))
-        ps_o = ctx.enter_context(tc.psum_pool(name="ps_o", bufs=4))
+        regrouped_pool = ctx.enter_context(tc.tile_pool(name="regrouped", bufs=AHEAD + 1))
+        quantised_pool = ctx.enter_context(tc.tile_pool(name="quantised", bufs=2))
+        out_pool = ctx.enter_context(
+            tc.tile_pool(name="out", bufs=ROUNDS // STORE_ROUNDS)
+        )
+        words_psum = ctx.enter_context(tc.psum_pool(name="words", bufs=4))
+        product_psum = ctx.enter_context(tc.psum_pool(name="product", bufs=ROUND))
 
-        srow = keep.tile([P, 64], BF16, name="srow")
-        nc.gpsimd.memset(srow[:], 0.0)
-        brow = keep.tile([P, N], BF16, name="brow")
-        nc.vector.memset(brow[:], 0.0)
+        dequant_row = keep.tile([P, DEQUANT_COLS], BF16, name="dequant_row")
+        nc.gpsimd.memset(dequant_row[:], 0.0)
+        bias_row = keep.tile([P, N], BF16, name="bias_row")
+        nc.vector.memset(bias_row[:], 0.0)
         ones = keep.tile([P, P], BF16, name="ones")
         nc.vector.memset(ones[:], 1.0)
-        ident = keep.tile([P, P], F32, name="ident")
-        make_identity(nc, ident[:])
+        identity = keep.tile([P, P], F32, name="identity")
+        make_identity(nc, identity[:])
 
-        q_sb = keep.tile([P, 4 * K], BF16, name="q_sb")
+        qw_sb = keep.tile([P, (N // P) * K], BF16, name="qw_sb")
         nc.sync.dma_start(
-            out=q_sb[:].rearrange("p (j k) -> p j k", j=4),
+            out=qw_sb[:].rearrange("p (j k) -> p j k", k=K),
             in_=qw.rearrange("(j p) k -> p j k", p=P),
         )
-        nc.sync.dma_start(out=srow[0:1, 0:1], in_=scale.unsqueeze(0))
-        nc.sync.dma_start(out=srow[0:1, 32:33], in_=zero_point.unsqueeze(0))
+        nc.sync.dma_start(
+            out=dequant_row[0:1, SCALE_COL : SCALE_COL + 1], in_=scale.unsqueeze(0)
+        )
+        nc.sync.dma_start(
+            out=dequant_row[0:1, ZERO_POINT_COL : ZERO_POINT_COL + 1],
+            in_=zero_point.unsqueeze(0),
+        )
         x_words = []
-        t0 = 0
-        for ci, cnt in enumerate(X_CHUNKS):
-            x_sb = keep.tile([P, cnt * K], BF16, name="x_sb%d" % ci)
-            nc.sync.dma_start(out=x_sb[:], in_=x2[:, t0 * K : (t0 + cnt) * K])
-            if ci == 0:
-                nc.sync.dma_start(out=brow[0:1, :], in_=bias.unsqueeze(0))
-            xw = x_sb[:].bitcast(F32)
-            for i in range(cnt):
-                x_words.append(xw[:, i * KW : (i + 1) * KW])
-            t0 += cnt
+        for i, tiles in enumerate(X_LOADS):
+            first = len(x_words)
+            x_sb = keep.tile([P, tiles * K], BF16, name="x_sb%d" % i)
+            nc.sync.dma_start(out=x_sb[:], in_=x_runs[:, first * K : (first + tiles) * K])
+            if i == 0:
+                nc.sync.dma_start(out=bias_row[0:1, :], in_=bias.unsqueeze(0))
+            x_sb_words = x_sb[:].bitcast(F32)
+            for t in range(tiles):
+                x_words.append(x_sb_words[:, t * WORDS : (t + 1) * WORDS])
 
-        sz_ps = ps_o.tile([P, 64], F32, name="sz_ps", tag="acc")
-        nc.tensor.matmul(sz_ps[:], lhsT=ones[:], rhs=srow[:], start=True, stop=True)
-        sz = keep.tile([P, 64], F32, name="sz")
-        nc.vector.tensor_copy(out=sz[:], in_=sz_ps[:])
-
-        q_words = q_sb[:].bitcast(F32)
-        w_grp = keep.tile([P, 4 * N], BF16, name="w_grp", align_bytes=64)
-        for h in range(2):
-            wt = ps_t.tile([P, 512], F32, name="wt", tag="tp")
+        def transpose_pair(bank, tile_words):
             for j in range(2):
                 for u in range(2):
-                    c0 = (2 * h + j) * KW + u * P
                     nc.tensor.transpose(
-                        wt[:, u * 256 + j * P : u * 256 + (j + 1) * P],
-                        q_words[:, c0 : c0 + P],
-                        ident[:],
+                        bank[:, HALF * u + P * j : HALF * u + P * (j + 1)],
+                        tile_words[j][:, P * u : P * (u + 1)],
+                        identity[:],
                     )
+
+        dequant_ps = product_psum.tile([P, DEQUANT_COLS], F32, name="dequant_ps", tag="product")
+        nc.tensor.matmul(dequant_ps[:], lhsT=ones[:], rhs=dequant_row[:], start=True, stop=True)
+        dequant = keep.tile([P, DEQUANT_COLS], F32, name="dequant")
+        nc.vector.tensor_copy(out=dequant[:], in_=dequant_ps[:])
+
+        qw_sb_words = qw_sb[:].bitcast(F32)
+        qw_words = []
+        for j in range(N // P):
+            qw_words.append(qw_sb_words[:, j * WORDS : (j + 1) * WORDS])
+        w_regrouped = keep.tile([P, PACK * N], BF16, name="w_regrouped", align_bytes=64)
+        for h in range(N // HALF):
+            bank = words_psum.tile([P, 2 * HALF], F32, name="w_bank", tag="words")
+            transpose_pair(bank, qw_words[2 * h : 2 * h + 2])
             nc.vector.tensor_scalar(
-                out=w_grp[:, h * 1024 : (h + 1) * 1024].rearrange(
+                out=w_regrouped[:, h * PACK * HALF : (h + 1) * PACK * HALF].rearrange(
                     "p (n u e) -> p n u e", u=2, e=2
                 ),
-                in0=wt[:].bitcast(BF16).rearrange("p (u n e) -> p n u e", u=2, e=2),
-                scalar1=sz[:, 32:33],
-                scalar2=sz[:, 0:1],
+                in0=bank[:].bitcast(BF16).rearrange("p (u n e) -> p n u e", u=2, e=2),
+                scalar1=dequant[:, ZERO_POINT_COL : ZERO_POINT_COL + 1],
+                scalar2=dequant[:, SCALE_COL : SCALE_COL + 1],
                 op0=ALU.subtract,
                 op1=ALU.mult,
             )
-        w_codes = keep.tile([P, N], U32, name="w_codes", align_bytes=64)
+        w_quads = keep.tile([P, N], U32, name="w_quads", align_bytes=64)
         w_scales = keep.tile([P, N], U8, name="w_scales", align_bytes=64)
         nc.vector.quantize_mx(
-            out=w_codes[:].bitcast(FP8X4), scales=w_scales[:], in_=w_grp[:]
+            out=w_quads[:].bitcast(FP8X4), scales=w_scales[:], in_=w_regrouped[:]
         )
 
-        b_ps = ps_o.tile([P, N], F32, name="b_ps", tag="acc")
-        nc.tensor.matmul(b_ps[:], lhsT=ones[:], rhs=brow[:], start=True, stop=True)
+        bias_ps = product_psum.tile([P, N], F32, name="bias_ps", tag="product")
+        nc.tensor.matmul(bias_ps[:], lhsT=ones[:], rhs=bias_row[:], start=True, stop=True)
         bias_sb = keep.tile([P, N], F32, name="bias_sb")
-        nc.scalar.copy(out=bias_sb[:], in_=b_ps[:])
+        nc.scalar.copy(out=bias_sb[:], in_=bias_ps[:])
 
-        grouped = {}
-        codes = {}
+        regrouped = {}
+        quantised = {}
 
-        def transposes(g):
-            grp = gpool.tile([P, GROUP * K], BF16, name="grp", align_bytes=64)
-            grouped[g] = grp
-            grp_w = grp[:].bitcast(F32)
-            for h in range(GROUP // 2):
-                xt = ps_t.tile([P, 512], F32, name="xt", tag="tp")
-                for j in range(2):
-                    xw = x_words[g * GROUP + 2 * h + j]
-                    for u in range(2):
-                        nc.tensor.transpose(
-                            xt[:, u * 256 + j * P : u * 256 + (j + 1) * P],
-                            xw[:, u * P : (u + 1) * P],
-                            ident[:],
-                        )
+        def transpose_round(g):
+            values = regrouped_pool.tile(
+                [P, ROUND * P * PACK], BF16, name="values", align_bytes=64
+            )
+            regrouped[g] = values
+            values_words = values[:].bitcast(F32)
+            for h in range(ROUND // 2):
+                bank = words_psum.tile([P, 2 * HALF], F32, name="x_bank", tag="words")
+                first = g * ROUND + 2 * h
+                transpose_pair(bank, x_words[first : first + 2])
                 nc.scalar.copy(
-                    out=grp_w[:, h * 512 : (h + 1) * 512].rearrange(
+                    out=values_words[:, h * 2 * HALF : (h + 1) * 2 * HALF].rearrange(
                         "p (r u) -> p r u", u=2
                     ),
-                    in_=xt[:].rearrange("p (u r) -> p r u", u=2),
+                    in_=bank[:].rearrange("p (u r) -> p r u", u=2),
                 )
 
-        def quantise(g):
-            cw = cpool.tile([P, GROUP * P], U32, name="cw", align_bytes=64)
-            cs = cpool.tile([P, GROUP * P], U8, name="cs", align_bytes=64)
-            codes[g] = (cw, cs)
+        def quantise_round(g):
+            quads = quantised_pool.tile([P, ROUND * P], U32, name="quads", align_bytes=64)
+            scales = quantised_pool.tile([P, ROUND * P], U8, name="scales", align_bytes=64)
+            quantised[g] = (quads, scales)
             nc.vector.quantize_mx(
-                out=cw[:].bitcast(FP8X4), scales=cs[:], in_=grouped[g][:]
+                out=quads[:].bitcast(FP8X4), scales=scales[:], in_=regrouped[g][:]
             )
 
-        for g in range(AHEAD):
-            transposes(g)
-        quantise(0)
-
-        store_i = 0
-        store_first = 0
-        store_cnt = 0
-        o_sb = None
-        for g in range(ROUNDS):
-            if g + AHEAD < ROUNDS:
-                transposes(g + AHEAD)
-            cw, cs = codes[g]
-            accs = []
-            for j in range(GROUP):
-                acc = ps_o.tile([P, N], F32, name="acc", tag="acc")
-                accs.append(acc)
+        def multiply_round(g):
+            quads, scales = quantised[g]
+            banks = []
+            for j in range(ROUND):
+                product = product_psum.tile([P, N], F32, name="product", tag="product")
+                banks.append(product)
                 nc.tensor.matmul_mx(
-                    out=acc[:],
-                    lhsT=cw[:, j * P : (j + 1) * P].bitcast(FP8X4),
-                    lhsT_scale=cs[:, j * P : (j + 1) * P],
-                    rhs=w_codes[:].bitcast(FP8X4),
+                    out=product[:],
+                    lhsT=quads[:, j * P : (j + 1) * P].bitcast(FP8X4),
+                    lhsT_scale=scales[:, j * P : (j + 1) * P],
+                    rhs=w_quads[:].bitcast(FP8X4),
                     rhs_scale=w_scales[:],
                     start=True,
                     stop=True,
                 )
-            if g + 1 < ROUNDS:
-                quantise(g + 1)
-            for j in range(GROUP):
-                t = g * GROUP + j
-                if t == store_first:
-                    store_cnt = STORE_TILES[store_i]
-                    o_sb = opool.tile([P, store_cnt * N], F32, name="o_sb")
-                c0 = (t - store_first) * N
-                if j in SCALAR_BANKS and g < ROUNDS - 1:
-                    nc.scalar.copy(out=o_sb[:, c0 : c0 + N], in_=accs[j][:])
+            return banks
+
+        def add_bias_round(banks, result):
+            for j in range(ROUND):
+                columns = result[:, j * N : (j + 1) * N]
+                if j == SCALAR_BANK:
+                    nc.scalar.copy(out=columns, in_=banks[j][:])
                     nc.gpsimd.tensor_tensor(
-                        out=o_sb[:, c0 : c0 + N],
-                        in0=o_sb[:, c0 : c0 + N],
-                        in1=bias_sb[:],
-                        op=ALU.add,
+                        out=columns, in0=columns, in1=bias_sb[:], op=ALU.add
                     )
                 else:
                     nc.vector.tensor_tensor(
-                        out=o_sb[:, c0 : c0 + N],
-                        in0=accs[j][:],
-                        in1=bias_sb[:],
-                        op=ALU.add,
+                        out=columns, in0=banks[j][:], in1=bias_sb[:], op=ALU.add
                     )
-                if t == store_first + store_cnt - 1:
-                    nc.sync.dma_start(
-                        out=out2[:, store_first * N : (t + 1) * N], in_=o_sb[:]
-                    )
-                    store_first = t + 1
-                    store_i += 1
+
+        for g in range(AHEAD):
+            transpose_round(g)
+        quantise_round(0)
+        out_sb = None
+        for g in range(ROUNDS):
+            if g + AHEAD < ROUNDS:
+                transpose_round(g + AHEAD)
+            banks = multiply_round(g)
+            if g + 1 < ROUNDS:
+                quantise_round(g + 1)
+            part = g % STORE_ROUNDS
+            if part == 0:
+                out_sb = out_pool.tile([P, STORE_ROUNDS * ROUND * N], F32, name="out_sb")
+            add_bias_round(banks, out_sb[:, part * ROUND * N : (part + 1) * ROUND * N])
+            if part == STORE_ROUNDS - 1:
+                last = (g + 1) * ROUND * N
+                nc.sync.dma_start(
+                    out=out_runs[:, last - STORE_ROUNDS * ROUND * N : last], in_=out_sb[:]
+                )

from contextlib import ExitStack

import concourse.mybir as mybir
from concourse.masks import make_identity

F32 = mybir.dt.float32
BF16 = mybir.dt.bfloat16
U32 = mybir.dt.uint32
U8 = mybir.dt.uint8
FP8X4 = mybir.dt.float8_e4m3fn_x4
ALU = mybir.AluOpType

P = 128
M, K, N = 8192, 512, 512
FLOPS = 2 * M * K * N
PACK = 4
WORDS = K // 2
HALF = 2 * P
ROW_TILES = M // P
ROUND = 4
ROUNDS = ROW_TILES // ROUND
AHEAD = 2
SCALAR_BANK = ROUND - 1
X_LOADS = (4, 4, 8, 16, 32)
STORE_ROUNDS = 2
SCALE_COL, ZERO_POINT_COL, DEQUANT_COLS = 0, 32, 64


def tile_quantizedlinear_t_kernel(tc, x, qw, scale, zero_point, bias, out):
    nc = tc.nc
    x_runs = x.rearrange("(p t) k -> p (t k)", t=ROW_TILES)
    out_runs = out.rearrange("(p t) n -> p (t n)", t=ROW_TILES)

    with ExitStack() as ctx:
        ctx.enter_context(tc.manual_schedule())
        keep = ctx.enter_context(tc.tile_pool(name="keep", bufs=1))
        regrouped_pool = ctx.enter_context(tc.tile_pool(name="regrouped", bufs=AHEAD + 1))
        quantised_pool = ctx.enter_context(tc.tile_pool(name="quantised", bufs=2))
        out_pool = ctx.enter_context(
            tc.tile_pool(name="out", bufs=ROUNDS // STORE_ROUNDS)
        )
        words_psum = ctx.enter_context(tc.psum_pool(name="words", bufs=4))
        product_psum = ctx.enter_context(tc.psum_pool(name="product", bufs=ROUND))

        dequant_row = keep.tile([P, DEQUANT_COLS], BF16, name="dequant_row")
        nc.gpsimd.memset(dequant_row[:], 0.0)
        bias_row = keep.tile([P, N], BF16, name="bias_row")
        nc.vector.memset(bias_row[:], 0.0)
        ones = keep.tile([P, P], BF16, name="ones")
        nc.vector.memset(ones[:], 1.0)
        identity = keep.tile([P, P], F32, name="identity")
        make_identity(nc, identity[:])

        qw_sb = keep.tile([P, (N // P) * K], BF16, name="qw_sb")
        nc.sync.dma_start(
            out=qw_sb[:].rearrange("p (j k) -> p j k", k=K),
            in_=qw.rearrange("(j p) k -> p j k", p=P),
        )
        nc.sync.dma_start(
            out=dequant_row[0:1, SCALE_COL : SCALE_COL + 1], in_=scale.unsqueeze(0)
        )
        nc.sync.dma_start(
            out=dequant_row[0:1, ZERO_POINT_COL : ZERO_POINT_COL + 1],
            in_=zero_point.unsqueeze(0),
        )
        x_words = []
        for i, tiles in enumerate(X_LOADS):
            first = len(x_words)
            x_sb = keep.tile([P, tiles * K], BF16, name="x_sb%d" % i)
            nc.sync.dma_start(out=x_sb[:], in_=x_runs[:, first * K : (first + tiles) * K])
            if i == 0:
                nc.sync.dma_start(out=bias_row[0:1, :], in_=bias.unsqueeze(0))
            x_sb_words = x_sb[:].bitcast(F32)
            for t in range(tiles):
                x_words.append(x_sb_words[:, t * WORDS : (t + 1) * WORDS])

        def transpose_pair(bank, tile_words):
            for j in range(2):
                for u in range(2):
                    nc.tensor.transpose(
                        bank[:, HALF * u + P * j : HALF * u + P * (j + 1)],
                        tile_words[j][:, P * u : P * (u + 1)],
                        identity[:],
                    )

        dequant_ps = product_psum.tile([P, DEQUANT_COLS], F32, name="dequant_ps", tag="product")
        nc.tensor.matmul(dequant_ps[:], lhsT=ones[:], rhs=dequant_row[:], start=True, stop=True)
        dequant = keep.tile([P, DEQUANT_COLS], F32, name="dequant")
        nc.vector.tensor_copy(out=dequant[:], in_=dequant_ps[:])

        qw_sb_words = qw_sb[:].bitcast(F32)
        qw_words = []
        for j in range(N // P):
            qw_words.append(qw_sb_words[:, j * WORDS : (j + 1) * WORDS])
        w_regrouped = keep.tile([P, PACK * N], BF16, name="w_regrouped", align_bytes=64)
        for h in range(N // HALF):
            bank = words_psum.tile([P, 2 * HALF], F32, name="w_bank", tag="words")
            transpose_pair(bank, qw_words[2 * h : 2 * h + 2])
            nc.vector.tensor_scalar(
                out=w_regrouped[:, h * PACK * HALF : (h + 1) * PACK * HALF].rearrange(
                    "p (n u e) -> p n u e", u=2, e=2
                ),
                in0=bank[:].bitcast(BF16).rearrange("p (u n e) -> p n u e", u=2, e=2),
                scalar1=dequant[:, ZERO_POINT_COL : ZERO_POINT_COL + 1],
                scalar2=dequant[:, SCALE_COL : SCALE_COL + 1],
                op0=ALU.subtract,
                op1=ALU.mult,
            )
        w_quads = keep.tile([P, N], U32, name="w_quads", align_bytes=64)
        w_scales = keep.tile([P, N], U8, name="w_scales", align_bytes=64)
        nc.vector.quantize_mx(
            out=w_quads[:].bitcast(FP8X4), scales=w_scales[:], in_=w_regrouped[:]
        )

        bias_ps = product_psum.tile([P, N], F32, name="bias_ps", tag="product")
        nc.tensor.matmul(bias_ps[:], lhsT=ones[:], rhs=bias_row[:], start=True, stop=True)
        bias_sb = keep.tile([P, N], F32, name="bias_sb")
        nc.scalar.copy(out=bias_sb[:], in_=bias_ps[:])

        regrouped = {}
        quantised = {}

        def transpose_round(g):
            values = regrouped_pool.tile(
                [P, ROUND * P * PACK], BF16, name="values", align_bytes=64
            )
            regrouped[g] = values
            values_words = values[:].bitcast(F32)
            for h in range(ROUND // 2):
                bank = words_psum.tile([P, 2 * HALF], F32, name="x_bank", tag="words")
                first = g * ROUND + 2 * h
                transpose_pair(bank, x_words[first : first + 2])
                nc.scalar.copy(
                    out=values_words[:, h * 2 * HALF : (h + 1) * 2 * HALF].rearrange(
                        "p (r u) -> p r u", u=2
                    ),
                    in_=bank[:].rearrange("p (u r) -> p r u", u=2),
                )

        def quantise_round(g):
            quads = quantised_pool.tile([P, ROUND * P], U32, name="quads", align_bytes=64)
            scales = quantised_pool.tile([P, ROUND * P], U8, name="scales", align_bytes=64)
            quantised[g] = (quads, scales)
            nc.vector.quantize_mx(
                out=quads[:].bitcast(FP8X4), scales=scales[:], in_=regrouped[g][:]
            )

        def multiply_round(g):
            quads, scales = quantised[g]
            banks = []
            for j in range(ROUND):
                product = product_psum.tile([P, N], F32, name="product", tag="product")
                banks.append(product)
                nc.tensor.matmul_mx(
                    out=product[:],
                    lhsT=quads[:, j * P : (j + 1) * P].bitcast(FP8X4),
                    lhsT_scale=scales[:, j * P : (j + 1) * P],
                    rhs=w_quads[:].bitcast(FP8X4),
                    rhs_scale=w_scales[:],
                    start=True,
                    stop=True,
                )
            return banks

        def add_bias_round(banks, result):
            for j in range(ROUND):
                columns = result[:, j * N : (j + 1) * N]
                if j == SCALAR_BANK:
                    nc.scalar.copy(out=columns, in_=banks[j][:])
                    nc.gpsimd.tensor_tensor(
                        out=columns, in0=columns, in1=bias_sb[:], op=ALU.add
                    )
                else:
                    nc.vector.tensor_tensor(
                        out=columns, in0=banks[j][:], in1=bias_sb[:], op=ALU.add
                    )

        for g in range(AHEAD):
            transpose_round(g)
        quantise_round(0)
        out_sb = None
        for g in range(ROUNDS):
            if g + AHEAD < ROUNDS:
                transpose_round(g + AHEAD)
            banks = multiply_round(g)
            if g + 1 < ROUNDS:
                quantise_round(g + 1)
            part = g % STORE_ROUNDS
            if part == 0:
                out_sb = out_pool.tile([P, STORE_ROUNDS * ROUND * N], F32, name="out_sb")
            add_bias_round(banks, out_sb[:, part * ROUND * N : (part + 1) * ROUND * N])
            if part == STORE_ROUNDS - 1:
                last = (g + 1) * ROUND * N
                nc.sync.dma_start(
                    out=out_runs[:, last - STORE_ROUNDS * ROUND * N : last], in_=out_sb[:]
                )
